import numpy as np
import ml_dtypes


def mxq(x, axis, fmt="e4m3"):
    dtype, down = {"e4m3": (ml_dtypes.float8_e4m3fn, 7), "e5m2": (ml_dtypes.float8_e5m2, 14)}[fmt]
    v = np.moveaxis(np.asarray(x, np.float32).astype(ml_dtypes.bfloat16).astype(np.float64), axis, -1)
    blocks = v.reshape(v.shape[:-1] + (-1, 32))
    amax = np.abs(blocks).max(-1, keepdims=True)
    byte = np.maximum(np.where(amax > 0, np.frexp(amax)[1] - 1 + 127, 0) - down, 1)
    scale = np.exp2(byte - 127.0)
    codes = (blocks / scale).astype(np.float32).astype(dtype).astype(np.float64)
    return np.moveaxis((codes * scale).reshape(v.shape), -1, axis)


WIDE = False


def mx_kscale(k):
    if not WIDE:
        return np.ones(k)
    levels = np.array([10, -10, 5, -5, 0])
    if k % 512:
        return np.exp2(np.random.permutation(np.resize(levels, k // 32))).repeat(32)
    a = np.empty((k // 512, 16))
    for p in range(k // 512):
        a[p, :8] = np.random.permutation(np.resize(levels, 8))
        for g in range(8):
            far = levels[np.abs(levels - a[p, g]) >= 10]
            a[p, g + 8] = far[np.random.randint(len(far))]
    return np.exp2(a.ravel()).repeat(32)


BF16 = ml_dtypes.bfloat16


def bf(x):
    return np.asarray(x, np.float32).astype(BF16)


def f64(x):
    return np.asarray(x).astype(np.float64)


B, GH, GW, E, H, DH = 256, 7, 7, 512, 4, 32
S = GH * GW
N = H * DH
BASE = 100.0


def rope_half(xh, ang):
    x1, x2 = xh[..., 0::2], xh[..., 1::2]
    cos = np.cos(ang)[None, :, None, :]
    sin = np.sin(ang)[None, :, None, :]
    o1 = x1 * cos - x2 * sin
    o2 = x1 * sin + x2 * cos
    return np.stack([o1, o2], axis=-1).reshape(xh.shape)


def rope_2d(t):
    dh = DH // 2
    rows = f64(np.repeat(np.arange(GH), GW))
    cols = f64(np.tile(np.arange(GW), GH))
    inv_freq = BASE ** (-f64(np.arange(0, dh, 2)) / dh)
    ang_r = rows[:, None] * inv_freq[None, :]
    ang_c = cols[:, None] * inv_freq[None, :]
    tr = rope_half(t[..., :dh], ang_r)
    tc = rope_half(t[..., dh:], ang_c)
    return np.concatenate([tr, tc], axis=-1)


def setup_inputs():
    s = mx_kscale(E)
    w = 1.0 / np.sqrt(E)
    return {"x": bf(np.random.standard_normal((B, S, E)) * s),
            "Wq": bf(np.random.standard_normal((E, N)) * w / s[:, None]),
            "bq": bf(np.random.standard_normal(N) * 0.3),
            "Wk": bf(np.random.standard_normal((E, N)) * w / s[:, None]),
            "bk": bf(np.random.standard_normal(N) * 0.3)}


def reference(x, Wq, bq, Wk, bk):
    xq = mxq(f64(x), 2, "e4m3")
    q = ((xq @ mxq(f64(Wq), 0, "e4m3")) + f64(bq)).reshape(B, S, H, DH)
    k = ((xq @ mxq(f64(Wk), 0, "e4m3")) + f64(bk)).reshape(B, S, H, DH)
    return rope_2d(q), rope_2d(k)

@@ -1,0 +1,297 @@
+from contextlib import ExitStack
+
+import concourse.bass as bass
+import concourse.mybir as mybir
+import concourse.tile as tile
+from concourse.masks import make_identity
+
+F32 = mybir.dt.float32
+BF16 = mybir.dt.bfloat16
+U32 = mybir.dt.uint32
+U8 = mybir.dt.uint8
+FP8X4 = mybir.dt.float8_e4m3fn_x4
+ALU = mybir.AluOpType
+ACT = mybir.ActivationFunctionType
+
+P = 128
+IMAGES = 256
+GRID = 7
+NPOS = GRID * GRID
+E = 512
+WORDS = E // 2
+NF = 128
+BASE = 100.0
+FLOPS = 2 * IMAGES * NPOS * E * 2 * NF
+
+X_CHUNKS = [2, 4, 6, 8, 8, 8, 8, 5]
+O_CHUNKS = [8, 8, 8, 8, 8, 4, 2, 2, 1]
+SCALAR_EVAC_EVERY = 4
+
+
+def cos_sin(theta):
+    c, s, term = 0.0, 0.0, 1.0
+    for n in range(0, 30, 2):
+        c += term
+        term = term * theta / (n + 1)
+        s += term
+        term = -term * theta / (n + 2)
+    return c, s
+
+
+def chunk_table(lens):
+    table = []
+    for c, n in enumerate(lens):
+        for i in range(n):
+            table.append((c, i))
+    return table
+
+
+def tile_attention_pa_t_kernel(tc, x, Wq, bq, Wk, bk, out_0, out_1):
+    nc = tc.nc
+    assert sum(X_CHUNKS) == NPOS and sum(O_CHUNKS) == NPOS
+    x_of = chunk_table(X_CHUNKS)
+    o_of = chunk_table(O_CHUNKS)
+    xv = x.rearrange("(p h) s k -> p h s k", h=2)
+    ov = [o.rearrange("(p h) s a d -> p h s (a d)", h=2) for o in (out_0, out_1)]
+    nslot = (NPOS + 1) // 2
+
+    with ExitStack() as ctx:
+        ctx.enter_context(tc.manual_schedule())
+        const = ctx.enter_context(tc.tile_pool(name="const", bufs=1))
+        xpool = ctx.enter_context(tc.tile_pool(name="xpool", bufs=1))
+        work = ctx.enter_context(tc.tile_pool(name="work", bufs=2))
+        opool = ctx.enter_context(tc.tile_pool(name="opool", bufs=3))
+        ps_x = ctx.enter_context(tc.psum_pool(name="ps_x", bufs=1))
+        ps_p = ctx.enter_context(tc.psum_pool(name="ps_p", bufs=2))
+        ps_o = ctx.enter_context(tc.psum_pool(name="ps_o", bufs=1))
+
+        wraw = const.tile([P, 2, 4, NF], BF16, name="wraw")
+        for q, w in enumerate((Wq, Wk)):
+            nc.scalar.dma_start(
+                out=wraw[:, q, :, :],
+                in_=w.rearrange("(p t) f -> p t f", t=4),
+            )
+        xs = []
+        s0 = 0
+        for c, n in enumerate(X_CHUNKS):
+            xt_sb = xpool.tile([P, 2 * n * E], BF16, name="xs%d" % c)
+            nc.sync.dma_start(
+                out=xt_sb[:].rearrange("p (h s k) -> p h s k", h=2, s=n),
+                in_=xv[:, :, s0 : s0 + n, :],
+            )
+            xs.append(xt_sb)
+            s0 += n
+
+        ident = const.tile([P, P], F32, name="ident")
+        make_identity(nc, ident[:])
+        warm = const.tile([P, 2], F32, name="warm")
+        nc.gpsimd.memset(warm[:, 0:1], 0.0)
+        nc.scalar.activation(out=warm[:, 1:2], in_=warm[:, 0:1], func=ACT.Identity)
+
+        rw = const.tile([P, 3, P], F32, name="rw")
+        nc.vector.memset(rw[:], 0.0)
+        bst = const.tile([P, 2 * NF], BF16, name="bst")
+        nc.vector.memset(bst[:], 0.0)
+        nc.scalar.dma_start(out=bst[0:1, 0:NF], in_=bq.unsqueeze(0))
+        nc.scalar.dma_start(out=bst[0:1, NF : 2 * NF], in_=bk.unsqueeze(0))
+        for j in range(8):
+            theta = BASE ** (-(2.0 * j) / 16.0)
+            for v, val in enumerate(cos_sin(theta)):
+                col = rw[:, v, :].rearrange("p (g j) -> p g j", j=8)[:, :, j]
+                nc.vector.tensor_scalar(out=col, in0=col, scalar1=val, scalar2=None, op0=ALU.add)
+        nc.vector.memset(rw[:, 2, :].rearrange("p (g h j) -> p g h j", h=2, j=8)[:, :, 1, :], 1.0)
+
+        pt = ps_o.tile([P, 512], F32, name="pt", tag="ot0")
+        for v in range(3):
+            nc.tensor.transpose(pt[:, v * P : (v + 1) * P], rw[:, v, :], ident[:])
+
+        wg = const.tile([P, 2, P, 4], BF16, name="wg", align_bytes=64)
+        for ab in range(2):
+            nc.scalar.copy(
+                out=wg[:, ab, :, :].rearrange("p (q r) t -> p q r t", q=2),
+                in_=wraw[:].rearrange("p q t (r b) -> p b q r t", b=2)[:, ab],
+            )
+        wc = const.tile([P, 2 * P], U32, name="wc", align_bytes=64)
+        ws = const.tile([P, 2 * P], U8, name="ws", align_bytes=64)
+
+        tcs = const.tile([P, 2, GRID], F32, name="tcs")
+        h01 = const.tile([P, 2], F32, name="h01")
+        nc.vector.memset(tcs[:, 0, 0:1], 1.0)
+        nc.vector.memset(tcs[:, 1, 0:1], 0.0)
+        ptv = pt[:].rearrange("p (v n) -> p v n", n=P)
+        nc.vector.tensor_copy(out=tcs[:, :, 1], in_=ptv[:, 0:2, 0])
+        nc.vector.tensor_copy(out=h01[:, 1:2], in_=ptv[:, 2, 0:1])
+        nc.vector.tensor_scalar(out=h01[:, 0:1], in0=h01[:, 1:2], scalar1=-1.0, scalar2=1.0,
+                                op0=ALU.mult, op1=ALU.add)
+
+        def add_angle(k, lo, hi):
+            ck = tcs[:, 0, k : k + 1]
+            sk = tcs[:, 1, k : k + 1]
+            n = hi - lo
+            u = const.tile([P, 2, 2], F32, name="u%d" % k)
+            nc.vector.tensor_scalar(out=u[:, :, 0:n], in0=tcs[:, :, lo:hi], scalar1=sk, scalar2=None,
+                                    op0=ALU.mult)
+            nc.vector.scalar_tensor_tensor(out=tcs[:, 0, lo + k : hi + k], in0=tcs[:, 0, lo:hi], scalar=ck,
+                                           in1=u[:, 1, 0:n], op0=ALU.mult, op1=ALU.subtract)
+            nc.vector.scalar_tensor_tensor(out=tcs[:, 1, lo + k : hi + k], in0=tcs[:, 1, lo:hi], scalar=ck,
+                                           in1=u[:, 0, 0:n], op0=ALU.mult, op1=ALU.add)
+
+        add_angle(1, 1, 2)
+        add_angle(2, 1, 3)
+        add_angle(4, 1, 3)
+
+        cos_t = const.tile([P, NPOS], F32, name="cos_t")
+        sin_t = const.tile([P, NPOS], F32, name="sin_t")
+        nsin_t = const.tile([P, NPOS], F32, name="nsin_t")
+        bias_a = const.tile([P, NPOS], F32, name="bias_a")
+        bias_b = const.tile([P, NPOS], F32, name="bias_b")
+        tmp0 = const.tile([P, NPOS], F32, name="tmp0")
+        tmp1 = const.tile([P, NPOS], F32, name="tmp1")
+        for v, (dst, tmp) in enumerate(((cos_t, tmp0), (sin_t, tmp1))):
+            by_col = tcs[:, v, :].unsqueeze(1).to_broadcast([P, GRID, GRID])
+            by_row = tcs[:, v, :].unsqueeze(2).to_broadcast([P, GRID, GRID])
+            tv = tmp[:].rearrange("p (r c) -> p r c", c=GRID)
+            nc.vector.tensor_scalar(out=tv, in0=by_col, scalar1=h01[:, 1:2], scalar2=None, op0=ALU.mult)
+            nc.vector.scalar_tensor_tensor(out=dst[:].rearrange("p (r c) -> p r c", c=GRID), in0=by_row,
+                                           scalar=h01[:, 0:1], in1=tv, op0=ALU.mult, op1=ALU.add)
+        nc.vector.tensor_scalar(out=nsin_t[:], in0=sin_t[:], scalar1=-1.0, scalar2=None, op0=ALU.mult)
+
+        nc.vector.quantize_mx(out=wc[:].bitcast(FP8X4), scales=ws[:],
+                              in_=wg[:].rearrange("p b m t -> p (b m t)"))
+
+        rwb = const.tile([P, 2, P], F32, name="rwb")
+        nc.vector.tensor_copy(out=rwb[:], in_=bst[:].rearrange("p (m b) -> p b m", b=2))
+        pt2 = ps_o.tile([P, 512], F32, name="pt2", tag="ot1")
+        bab = const.tile([P, 2], F32, name="bab")
+        tmp2 = const.tile([P, NPOS], F32, name="tmp2")
+        tmp3 = const.tile([P, NPOS], F32, name="tmp3")
+
+        def bias_transposes():
+            for v in range(2):
+                nc.tensor.transpose(pt2[:, v * P : (v + 1) * P], rwb[:, v, :], ident[:])
+
+        def bias_tables():
+            nc.vector.tensor_copy(out=bab[:], in_=pt2[:].rearrange("p (v n) -> p v n", n=P)[:, 0:2, 0])
+            nc.vector.tensor_scalar(out=tmp2[:], in0=sin_t[:], scalar1=bab[:, 1:2], scalar2=None, op0=ALU.mult)
+            nc.vector.scalar_tensor_tensor(out=bias_a[:], in0=cos_t[:], scalar=bab[:, 0:1], in1=tmp2[:],
+                                           op0=ALU.mult, op1=ALU.subtract)
+            nc.vector.tensor_scalar(out=tmp3[:], in0=cos_t[:], scalar1=bab[:, 1:2], scalar2=None, op0=ALU.mult)
+            nc.vector.scalar_tensor_tensor(out=bias_b[:], in0=sin_t[:], scalar=bab[:, 0:1], in1=tmp3[:],
+                                           op0=ALU.mult, op1=ALU.add)
+
+        st = {}
+
+        def positions(n):
+            return [s for s in (2 * n, 2 * n + 1) if s < NPOS]
+
+        def stage_l(n):
+            for j, s in enumerate(positions(n)):
+                c, i = x_of[s]
+                x32 = xs[c][:].bitcast(F32)
+                xt = ps_x.tile([P, 512], F32, name="xt", tag="xt%d" % j)
+                for h in range(2):
+                    for u in range(2):
+                        off = (h * X_CHUNKS[c] + i) * WORDS
+                        nc.tensor.transpose(xt[:, (2 * h + u) * P : (2 * h + u + 1) * P],
+                                            x32[:, off + u : off + WORDS : 2], ident[:])
+                st["xt", s] = xt
+
+        def stage_e(n):
+            pos = positions(n)
+            xg = work.tile([P, 2048], BF16, name="xg", align_bytes=64)
+            st["xg", n] = xg
+            for j, s in enumerate(pos):
+                dst = xg[:, j * 1024 : (j + 1) * 1024].bitcast(F32).rearrange("p (h i u) -> p h i u", h=2, u=2)
+                src = st["xt", s][:].rearrange("p (h u i) -> p h i u", h=2, u=2)
+                if s % SCALAR_EVAC_EVERY == 1:
+                    nc.scalar.copy(out=dst, in_=src)
+                else:
+                    nc.vector.tensor_copy(out=dst, in_=src)
+
+        def stage_q(n):
+            w = 256 * len(positions(n))
+            xc = work.tile([P, 512], U32, name="xc", align_bytes=64)
+            xsc = work.tile([P, 512], U8, name="xsc", align_bytes=64)
+            nc.vector.quantize_mx(out=xc[:, 0:w].bitcast(FP8X4), scales=xsc[:, 0:w], in_=st["xg", n][:, 0 : 4 * w])
+            st["xc", n] = (xc, xsc)
+
+        def stage_m(n):
+            xc, xsc = st["xc", n]
+            for j, s in enumerate(positions(n)):
+                pp = ps_p.tile([P, 512], F32, name="pp", tag="pp%d" % j)
+                for ab in range(2):
+                    nc.tensor.matmul_mx(
+                        out=pp[:, ab * 256 : (ab + 1) * 256],
+                        lhsT=wc[:, ab * P : (ab + 1) * P].bitcast(FP8X4),
+                        lhsT_scale=ws[:, ab * P : (ab + 1) * P],
+                        rhs=xc[:, j * 256 : (j + 1) * 256].bitcast(FP8X4),
+                        rhs_scale=xsc[:, j * 256 : (j + 1) * 256],
+                        start=True,
+                        stop=True,
+                    )
+                st["pp", s] = pp
+
+        def stage_a(n):
+            for j, s in enumerate(positions(n)):
+                pp = st["pp", s]
+                tt = work.tile([P, 512], F32, name="tt", tag="tt%d" % j)
+                nc.scalar.activation(out=tt[:, 256:512], in_=pp[:, 256:512], func=ACT.Identity,
+                                     bias=bias_b[:, s : s + 1], scale=cos_t[:, s : s + 1])
+                nc.scalar.activation(out=tt[:, 0:256], in_=pp[:, 0:256], func=ACT.Identity,
+                                     bias=bias_a[:, s : s + 1], scale=cos_t[:, s : s + 1])
+                st["tt", s] = tt
+
+        def stage_b(n):
+            for j, s in enumerate(positions(n)):
+                pp = st["pp", s]
+                tt = st["tt", s]
+                oo = work.tile([P, 512], F32, name="oo", tag="oo%d" % j)
+                nc.vector.scalar_tensor_tensor(out=oo[:, 0:256], in0=pp[:, 256:512], scalar=nsin_t[:, s : s + 1],
+                                               in1=tt[:, 0:256], op0=ALU.mult, op1=ALU.add)
+                nc.vector.scalar_tensor_tensor(out=oo[:, 256:512], in0=pp[:, 0:256], scalar=sin_t[:, s : s + 1],
+                                               in1=tt[:, 256:512], op0=ALU.mult, op1=ALU.add)
+                st["oo", s] = oo
+
+        def stage_t(n):
+            for j, s in enumerate(positions(n)):
+                oo = st["oo", s]
+                ot = ps_o.tile([P, 512], F32, name="ot", tag="ot%d" % j)
+                for g in range(4):
+                    nc.tensor.transpose(ot[:, g * P : (g + 1) * P], oo[:, g * P : (g + 1) * P], ident[:])
+                st["ot", s] = ot
+
+        def stage_c(n):
+            for s in positions(n):
+                c, i = o_of[s]
+                ln = O_CHUNKS[c]
+                if i == 0:
+                    st["ob", c] = [opool.tile([P, 2 * 8 * NF], F32, name="ob%d" % q) for q in range(2)]
+                src = st["ot", s][:].rearrange("p (b h q m) -> p q h m b", b=2, h=2, q=2)
+                for q in range(2):
+                    dst = st["ob", c][q][:, 0 : 2 * ln * NF].rearrange("p (h s m b) -> p h s m b", h=2, s=ln, b=2)
+                    nc.scalar.copy(out=dst[:, :, i, :, :], in_=src[:, q])
+                if i == ln - 1:
+                    first = s - i
+                    for q in range(2):
+                        nc.sync.dma_start(
+                            out=ov[q][:, :, first : first + ln, :],
+                            in_=st["ob", c][q][:, 0 : 2 * ln * NF].rearrange("p (h s f) -> p h s f", h=2, s=ln),
+                        )
+
+        def run(stage, n):
+            if 0 <= n < nslot:
+                stage(n)
+
+        for t in range(-1, nslot + 2):
+            run(stage_l, t + 1)
+            if t == -1:
+                bias_transposes()
+            run(stage_q, t)
+            if t == 0:
+                bias_tables()
+            run(stage_a, t - 1)
+            run(stage_e, t + 1)
+            run(stage_t, t - 2)
+            run(stage_b, t - 1)
+            run(stage_c, t - 2)
+            run(stage_m, t)

@@ -65,9 +65,12 @@ def tile_attention_pa_t_kernel(tc, x, Wq, bq, Wk, bk, out_0, out_1):
         ps_p = ctx.enter_context(tc.psum_pool(name="ps_p", bufs=2))
         ps_o = ctx.enter_context(tc.psum_pool(name="ps_o", bufs=1))
 
+        bpair = const.tile([P, 2], BF16, name="bpair")
+        for q, b in enumerate((bq, bk)):
+            nc.sync.dma_start(out=bpair[64 * q : 64 * (q + 1), :], in_=b.rearrange("(m e) -> m e", e=2))
         wraw = const.tile([P, 2, 4, NF], BF16, name="wraw")
         for q, w in enumerate((Wq, Wk)):
-            nc.scalar.dma_start(
+            nc.sync.dma_start(
                 out=wraw[:, q, :, :],
                 in_=w.rearrange("(p t) f -> p t f", t=4),
             )
@@ -90,10 +93,6 @@ def tile_attention_pa_t_kernel(tc, x, Wq, bq, Wk, bk, out_0, out_1):
 
         rw = const.tile([P, 3, P], F32, name="rw")
         nc.vector.memset(rw[:], 0.0)
-        bst = const.tile([P, 2 * NF], BF16, name="bst")
-        nc.vector.memset(bst[:], 0.0)
-        nc.scalar.dma_start(out=bst[0:1, 0:NF], in_=bq.unsqueeze(0))
-        nc.scalar.dma_start(out=bst[0:1, NF : 2 * NF], in_=bk.unsqueeze(0))
         for j in range(8):
             theta = BASE ** (-(2.0 * j) / 16.0)
             for v, val in enumerate(cos_sin(theta)):
@@ -140,6 +139,9 @@ def tile_attention_pa_t_kernel(tc, x, Wq, bq, Wk, bk, out_0, out_1):
         add_angle(2, 1, 3)
         add_angle(4, 1, 3)
 
+        nc.vector.quantize_mx(out=wc[:].bitcast(FP8X4), scales=ws[:],
+                              in_=wg[:].rearrange("p b m t -> p (b m t)"))
+
         cos_t = const.tile([P, NPOS], F32, name="cos_t")
         sin_t = const.tile([P, NPOS], F32, name="sin_t")
         nsin_t = const.tile([P, NPOS], F32, name="nsin_t")
@@ -156,22 +158,12 @@ def tile_attention_pa_t_kernel(tc, x, Wq, bq, Wk, bk, out_0, out_1):
                                            scalar=h01[:, 0:1], in1=tv, op0=ALU.mult, op1=ALU.add)
         nc.vector.tensor_scalar(out=nsin_t[:], in0=sin_t[:], scalar1=-1.0, scalar2=None, op0=ALU.mult)
 
-        nc.vector.quantize_mx(out=wc[:].bitcast(FP8X4), scales=ws[:],
-                              in_=wg[:].rearrange("p b m t -> p (b m t)"))
-
-        rwb = const.tile([P, 2, P], F32, name="rwb")
-        nc.vector.tensor_copy(out=rwb[:], in_=bst[:].rearrange("p (m b) -> p b m", b=2))
-        pt2 = ps_o.tile([P, 512], F32, name="pt2", tag="ot1")
         bab = const.tile([P, 2], F32, name="bab")
         tmp2 = const.tile([P, NPOS], F32, name="tmp2")
         tmp3 = const.tile([P, NPOS], F32, name="tmp3")
 
-        def bias_transposes():
-            for v in range(2):
-                nc.tensor.transpose(pt2[:, v * P : (v + 1) * P], rwb[:, v, :], ident[:])
-
         def bias_tables():
-            nc.vector.tensor_copy(out=bab[:], in_=pt2[:].rearrange("p (v n) -> p v n", n=P)[:, 0:2, 0])
+            nc.vector.tensor_copy(out=bab[:], in_=bpair[:])
             nc.vector.tensor_scalar(out=tmp2[:], in0=sin_t[:], scalar1=bab[:, 1:2], scalar2=None, op0=ALU.mult)
             nc.vector.scalar_tensor_tensor(out=bias_a[:], in0=cos_t[:], scalar=bab[:, 0:1], in1=tmp2[:],
                                            op0=ALU.mult, op1=ALU.subtract)
@@ -203,7 +195,7 @@ def tile_attention_pa_t_kernel(tc, x, Wq, bq, Wk, bk, out_0, out_1):
             for j, s in enumerate(pos):
                 dst = xg[:, j * 1024 : (j + 1) * 1024].bitcast(F32).rearrange("p (h i u) -> p h i u", h=2, u=2)
                 src = st["xt", s][:].rearrange("p (h u i) -> p h i u", h=2, u=2)
-                if s % SCALAR_EVAC_EVERY == 1:
+                if s % SCALAR_EVAC_EVERY == 1 or n == 0:
                     nc.scalar.copy(out=dst, in_=src)
                 else:
                     nc.vector.tensor_copy(out=dst, in_=src)
@@ -284,8 +276,6 @@ def tile_attention_pa_t_kernel(tc, x, Wq, bq, Wk, bk, out_0, out_1):
 
         for t in range(-1, nslot + 2):
             run(stage_l, t + 1)
-            if t == -1:
-                bias_transposes()
             run(stage_q, t)
             if t == 0:
                 bias_tables()

@@ -23,9 +23,24 @@ NF = 128
 BASE = 100.0
 FLOPS = 2 * IMAGES * NPOS * E * 2 * NF
 
-X_CHUNKS = [2, 4, 6, 8, 8, 8, 8, 5]
-O_CHUNKS = [8, 8, 8, 8, 8, 4, 2, 2, 1]
-SCALAR_EVAC_EVERY = 4
+def slot_list():
+    slots = []
+    for row in range(1, GRID):
+        s7 = GRID * row
+        slots += [(s7 + 1, s7 + 2), (s7 + 3, s7), (s7 + 4, s7 + 5), (s7 + 6, row)]
+    return slots + [(0,)]
+
+
+SLOTS = slot_list()
+
+X_CHUNKS = [(8, 2), (7, 1), (10, 2), (12, 2), (1, 1), (14, 7), (2, 5), (21, 7), (28, 7), (35, 7), (42, 7), (0, 1)]
+
+
+SCALAR_COPY = {False: (False, True), True: (False, True)}
+
+
+def is_edge(s):
+    return s < GRID or s % GRID == 0
 
 
 def cos_sin(theta):
@@ -38,22 +53,29 @@ def cos_sin(theta):
     return c, s
 
 
-def chunk_table(lens):
-    table = []
-    for c, n in enumerate(lens):
+def store_groups():
+    groups = []
+    for row in range(1, GRID):
+        groups += [(GRID * row, 4), (GRID * row + 4, 3)]
+    groups += [(1, 3), (4, 3), (0, 1)]
+    of = {}
+    for g, (first, n) in enumerate(groups):
         for i in range(n):
-            table.append((c, i))
-    return table
+            of[first + i] = (g, i)
+    return groups, of
 
 
 def tile_attention_pa_t_kernel(tc, x, Wq, bq, Wk, bk, out_0, out_1):
     nc = tc.nc
-    assert sum(X_CHUNKS) == NPOS and sum(O_CHUNKS) == NPOS
-    x_of = chunk_table(X_CHUNKS)
-    o_of = chunk_table(O_CHUNKS)
+    x_of = {}
+    for c, (first, n) in enumerate(X_CHUNKS):
+        for i in range(n):
+            x_of[first + i] = (c, i)
+    groups, o_of = store_groups()
+    assert len(x_of) == NPOS and len(o_of) == NPOS
     xv = x.rearrange("(p h) s k -> p h s k", h=2)
     ov = [o.rearrange("(p h) s a d -> p h s (a d)", h=2) for o in (out_0, out_1)]
-    nslot = (NPOS + 1) // 2
+    nslot = len(SLOTS)
 
     with ExitStack() as ctx:
         ctx.enter_context(tc.manual_schedule())
@@ -70,20 +92,15 @@ def tile_attention_pa_t_kernel(tc, x, Wq, bq, Wk, bk, out_0, out_1):
             nc.sync.dma_start(out=bpair[64 * q : 64 * (q + 1), :], in_=b.rearrange("(m e) -> m e", e=2))
         wraw = const.tile([P, 2, 4, NF], BF16, name="wraw")
         for q, w in enumerate((Wq, Wk)):
-            nc.sync.dma_start(
-                out=wraw[:, q, :, :],
-                in_=w.rearrange("(p t) f -> p t f", t=4),
-            )
+            nc.sync.dma_start(out=wraw[:, q, :, :], in_=w.rearrange("(p t) f -> p t f", t=4))
         xs = []
-        s0 = 0
-        for c, n in enumerate(X_CHUNKS):
+        for c, (first, n) in enumerate(X_CHUNKS):
             xt_sb = xpool.tile([P, 2 * n * E], BF16, name="xs%d" % c)
             nc.sync.dma_start(
                 out=xt_sb[:].rearrange("p (h s k) -> p h s k", h=2, s=n),
-                in_=xv[:, :, s0 : s0 + n, :],
+                in_=xv[:, :, first : first + n, :],
             )
             xs.append(xt_sb)
-            s0 += n
 
         ident = const.tile([P, P], F32, name="ident")
         make_identity(nc, ident[:])
@@ -103,6 +120,42 @@ def tile_attention_pa_t_kernel(tc, x, Wq, bq, Wk, bk, out_0, out_1):
         pt = ps_o.tile([P, 512], F32, name="pt", tag="ot0")
         for v in range(3):
             nc.tensor.transpose(pt[:, v * P : (v + 1) * P], rw[:, v, :], ident[:])
+
+        wgn = const.tile([P, 2 * NF, 4], BF16, name="wgn", align_bytes=64)
+        nc.gpsimd.tensor_scalar(
+            out=wgn[:].rearrange("p (q f) t -> p q f t", q=2),
+            in0=wraw[:].rearrange("p q t f -> p q f t"),
+            scalar1=1.0, scalar2=0.0, op0=ALU.mult, op1=ALU.add)
+        wcn = const.tile([P, 2 * P], U32, name="wcn", align_bytes=64)
+        wsn = const.tile([P, 2 * P], U8, name="wsn", align_bytes=64)
+
+        gx = const.tile([P, 2, GRID, 8], F32, name="gx")
+        nc.gpsimd.memset(gx[:, 0, 0, :], 1.0)
+        nc.gpsimd.memset(gx[:, 1, 0, :], 0.0)
+        nc.gpsimd.tensor_copy(out=gx[:, :, 1, :], in_=rw[:, 0:2, 0:8])
+
+        def add_angle_free(k, lo, hi):
+            n = hi - lo
+            prod = []
+            for v in range(2):
+                t = const.tile([P, 2, 2, 8], F32, name="g%d_%d" % (k, v))
+                nc.gpsimd.tensor_tensor(
+                    out=t[:, :, 0:n, :], in0=gx[:, :, lo:hi, :],
+                    in1=gx[:, v, k, :].unsqueeze(1).unsqueeze(1).to_broadcast([P, 2, n, 8]), op=ALU.mult)
+                prod.append(t)
+            nc.gpsimd.tensor_tensor(out=gx[:, 0, lo + k : hi + k, :], in0=prod[0][:, 0, 0:n, :],
+                                    in1=prod[1][:, 1, 0:n, :], op=ALU.subtract)
+            nc.gpsimd.tensor_tensor(out=gx[:, 1, lo + k : hi + k, :], in0=prod[0][:, 1, 0:n, :],
+                                    in1=prod[1][:, 0, 0:n, :], op=ALU.add)
+
+        add_angle_free(1, 1, 2)
+        add_angle_free(2, 1, 3)
+        add_angle_free(4, 1, 3)
+        cx = const.tile([P, GRID, 8, 2], F32, name="cx")
+        sx = const.tile([P, GRID, 8, 2], F32, name="sx")
+        nc.gpsimd.tensor_copy(out=cx[:], in_=gx[:, 0].unsqueeze(3).to_broadcast([P, GRID, 8, 2]))
+        nc.gpsimd.tensor_scalar(out=sx[:, :, :, 0], in0=gx[:, 1], scalar1=-1.0, scalar2=None, op0=ALU.mult)
+        nc.gpsimd.tensor_copy(out=sx[:, :, :, 1], in_=gx[:, 1])
 
         wg = const.tile([P, 2, P, 4], BF16, name="wg", align_bytes=64)
         for ab in range(2):
@@ -161,9 +214,11 @@ def tile_attention_pa_t_kernel(tc, x, Wq, bq, Wk, bk, out_0, out_1):
         bab = const.tile([P, 2], F32, name="bab")
         tmp2 = const.tile([P, NPOS], F32, name="tmp2")
         tmp3 = const.tile([P, NPOS], F32, name="tmp3")
+        nc.vector.tensor_copy(out=bab[:], in_=bpair[:])
+        pt2 = ps_o.tile([P, 512], F32, name="pt2", tag="ot1")
+        bias_row = const.tile([P, 2, P, 2], F32, name="bias_row")
 
         def bias_tables():
-            nc.vector.tensor_copy(out=bab[:], in_=bpair[:])
             nc.vector.tensor_scalar(out=tmp2[:], in0=sin_t[:], scalar1=bab[:, 1:2], scalar2=None, op0=ALU.mult)
             nc.vector.scalar_tensor_tensor(out=bias_a[:], in0=cos_t[:], scalar=bab[:, 0:1], in1=tmp2[:],
                                            op0=ALU.mult, op1=ALU.subtract)
@@ -171,37 +226,45 @@ def tile_attention_pa_t_kernel(tc, x, Wq, bq, Wk, bk, out_0, out_1):
             nc.vector.scalar_tensor_tensor(out=bias_b[:], in0=sin_t[:], scalar=bab[:, 0:1], in1=tmp3[:],
                                            op0=ALU.mult, op1=ALU.add)
 
+        def edge_tables():
+            nc.vector.quantize_mx(out=wcn[:].bitcast(FP8X4), scales=wsn[:],
+                                  in_=wgn[:].rearrange("p f t -> p (f t)"))
+            nc.vector.tensor_copy(
+                out=bias_row[:],
+                in_=pt2[:, 0 : 2 * P].rearrange("p (e m) -> p m e", e=2).unsqueeze(1).to_broadcast([P, 2, P, 2]))
+
         st = {}
 
-        def positions(n):
-            return [s for s in (2 * n, 2 * n + 1) if s < NPOS]
-
         def stage_l(n):
-            for j, s in enumerate(positions(n)):
+            for j, s in enumerate(SLOTS[n]):
                 c, i = x_of[s]
                 x32 = xs[c][:].bitcast(F32)
                 xt = ps_x.tile([P, 512], F32, name="xt", tag="xt%d" % j)
                 for h in range(2):
                     for u in range(2):
-                        off = (h * X_CHUNKS[c] + i) * WORDS
+                        off = (h * X_CHUNKS[c][1] + i) * WORDS
                         nc.tensor.transpose(xt[:, (2 * h + u) * P : (2 * h + u + 1) * P],
                                             x32[:, off + u : off + WORDS : 2], ident[:])
                 st["xt", s] = xt
 
+        def on_scalar(n, j):
+            if n == 0:
+                return True
+            return SCALAR_COPY[any(is_edge(s) for s in SLOTS[n])][j]
+
         def stage_e(n):
-            pos = positions(n)
             xg = work.tile([P, 2048], BF16, name="xg", align_bytes=64)
             st["xg", n] = xg
-            for j, s in enumerate(pos):
+            for j, s in enumerate(SLOTS[n]):
                 dst = xg[:, j * 1024 : (j + 1) * 1024].bitcast(F32).rearrange("p (h i u) -> p h i u", h=2, u=2)
                 src = st["xt", s][:].rearrange("p (h u i) -> p h i u", h=2, u=2)
-                if s % SCALAR_EVAC_EVERY == 1 or n == 0:
+                if on_scalar(n, j):
                     nc.scalar.copy(out=dst, in_=src)
                 else:
                     nc.vector.tensor_copy(out=dst, in_=src)
 
         def stage_q(n):
-            w = 256 * len(positions(n))
+            w = 256 * len(SLOTS[n])
             xc = work.tile([P, 512], U32, name="xc", align_bytes=64)
             xsc = work.tile([P, 512], U8, name="xsc", align_bytes=64)
             nc.vector.quantize_mx(out=xc[:, 0:w].bitcast(FP8X4), scales=xsc[:, 0:w], in_=st["xg", n][:, 0 : 4 * w])
@@ -209,22 +272,25 @@ def tile_attention_pa_t_kernel(tc, x, Wq, bq, Wk, bk, out_0, out_1):
 
         def stage_m(n):
             xc, xsc = st["xc", n]
-            for j, s in enumerate(positions(n)):
+            for j, s in enumerate(SLOTS[n]):
                 pp = ps_p.tile([P, 512], F32, name="pp", tag="pp%d" % j)
-                for ab in range(2):
-                    nc.tensor.matmul_mx(
-                        out=pp[:, ab * 256 : (ab + 1) * 256],
-                        lhsT=wc[:, ab * P : (ab + 1) * P].bitcast(FP8X4),
-                        lhsT_scale=ws[:, ab * P : (ab + 1) * P],
-                        rhs=xc[:, j * 256 : (j + 1) * 256].bitcast(FP8X4),
-                        rhs_scale=xsc[:, j * 256 : (j + 1) * 256],
-                        start=True,
-                        stop=True,
-                    )
+                for g in range(2):
+                    if is_edge(s):
+                        cols = slice(j * 256 + g * P, j * 256 + (g + 1) * P)
+                        lhs, lhs_s = xc[:, cols], xsc[:, cols]
+                        rhs, rhs_s = wcn[:], wsn[:]
+                    else:
+                        cols = slice(j * 256, (j + 1) * 256)
+                        lhs, lhs_s = wc[:, g * P : (g + 1) * P], ws[:, g * P : (g + 1) * P]
+                        rhs, rhs_s = xc[:, cols], xsc[:, cols]
+                    nc.tensor.matmul_mx(out=pp[:, g * 256 : (g + 1) * 256], lhsT=lhs.bitcast(FP8X4), lhsT_scale=lhs_s,
+                                        rhs=rhs.bitcast(FP8X4), rhs_scale=rhs_s, start=True, stop=True)
                 st["pp", s] = pp
 
         def stage_a(n):
-            for j, s in enumerate(positions(n)):
+            for j, s in enumerate(SLOTS[n]):
+                if is_edge(s):
+                    continue
                 pp = st["pp", s]
                 tt = work.tile([P, 512], F32, name="tt", tag="tt%d" % j)
                 nc.scalar.activation(out=tt[:, 256:512], in_=pp[:, 256:512], func=ACT.Identity,
@@ -233,42 +299,82 @@ def tile_attention_pa_t_kernel(tc, x, Wq, bq, Wk, bk, out_0, out_1):
                                      bias=bias_a[:, s : s + 1], scale=cos_t[:, s : s + 1])
                 st["tt", s] = tt
 
+        def out_tile(s):
+            g, i = o_of[s]
+            n = groups[g][1]
+            if ("ob", g) not in st:
+                st["ob", g] = opool.tile([P, 4 * n * NF], F32, name="ob", tag="ob%d_%d" % (n, s < GRID))
+            return st["ob", g][:].rearrange("p (g s f) -> p g s f", g=4, s=n)[:, :, i, :]
+
         def stage_b(n):
-            for j, s in enumerate(positions(n)):
+            for j, s in enumerate(SLOTS[n]):
                 pp = st["pp", s]
-                tt = st["tt", s]
-                oo = work.tile([P, 512], F32, name="oo", tag="oo%d" % j)
-                nc.vector.scalar_tensor_tensor(out=oo[:, 0:256], in0=pp[:, 256:512], scalar=nsin_t[:, s : s + 1],
-                                               in1=tt[:, 0:256], op0=ALU.mult, op1=ALU.add)
-                nc.vector.scalar_tensor_tensor(out=oo[:, 256:512], in0=pp[:, 0:256], scalar=sin_t[:, s : s + 1],
-                                               in1=tt[:, 256:512], op0=ALU.mult, op1=ALU.add)
-                st["oo", s] = oo
+                if not is_edge(s):
+                    tt = st["tt", s]
+                    oo = work.tile([P, 512], F32, name="oo", tag="oo%d" % j)
+                    nc.vector.scalar_tensor_tensor(out=oo[:, 0:256], in0=pp[:, 256:512], scalar=nsin_t[:, s : s + 1],
+                                                   in1=tt[:, 0:256], op0=ALU.mult, op1=ALU.add)
+                    nc.vector.scalar_tensor_tensor(out=oo[:, 256:512], in0=pp[:, 0:256], scalar=sin_t[:, s : s + 1],
+                                                   in1=tt[:, 256:512], op0=ALU.mult, op1=ALU.add)
+                    st["oo", s] = oo
+                    continue
+                ob = out_tile(s)
+                brow = bias_row[:].rearrange("p h m e -> p (h m e)")
+                if s == 0:
+                    nc.vector.tensor_tensor(out=ob, in0=pp[:].rearrange("p (g f) -> p g f", g=4),
+                                            in1=brow.rearrange("p (g f) -> p g f", g=4), op=ALU.add)
+                    continue
+                rot = 1 if s < GRID else 0
+                angle = s if s < GRID else s // GRID
+                zr = work.tile([P, 256], F32, name="zr")
+                nc.vector.tensor_tensor(
+                    out=zr[:].rearrange("p (g f) -> p g f", f=16),
+                    in0=pp[:].rearrange("p (g v f) -> p g v f", v=2, f=16)[:, :, rot, :],
+                    in1=brow.rearrange("p (g v f) -> p g v f", v=2, f=16)[:, :, rot, :], op=ALU.add)
+                obv = ob.rearrange("p g (a v f) -> p g a v f", v=2, f=16)
+                nc.vector.tensor_tensor(
+                    out=obv[:, :, :, 1 - rot, :],
+                    in0=pp[:].rearrange("p (g a v f) -> p g a v f", g=4, v=2, f=16)[:, :, :, 1 - rot, :],
+                    in1=brow.rearrange("p (g a v f) -> p g a v f", g=4, v=2, f=16)[:, :, :, 1 - rot, :], op=ALU.add)
+                t1 = work.tile([P, 256], F32, name="t1")
+                t2 = work.tile([P, 256], F32, name="t2")
+                nc.gpsimd.tensor_tensor(
+                    out=t1[:].rearrange("p (g f) -> p g f", f=16),
+                    in0=zr[:].rearrange("p (g f) -> p g f", f=16),
+                    in1=cx[:, angle].rearrange("p j e -> p (j e)").unsqueeze(1).to_broadcast([P, 16, 16]), op=ALU.mult)
+                nc.gpsimd.tensor_tensor(
+                    out=t2[:].rearrange("p (g j e) -> p g j e", j=8, e=2),
+                    in0=zr[:].rearrange("p (g j e) -> p g j e", j=8, e=2)[:, :, :, ::-1],
+                    in1=sx[:, angle].unsqueeze(1).to_broadcast([P, 16, 8, 2]), op=ALU.mult)
+                nc.gpsimd.tensor_tensor(
+                    out=obv[:, :, :, rot, :],
+                    in0=t1[:].rearrange("p (g a f) -> p g a f", g=4, f=16),
+                    in1=t2[:].rearrange("p (g a f) -> p g a f", g=4, f=16), op=ALU.add)
 
         def stage_t(n):
-            for j, s in enumerate(positions(n)):
+            for j, s in enumerate(SLOTS[n]):
+                if is_edge(s):
+                    continue
                 oo = st["oo", s]
                 ot = ps_o.tile([P, 512], F32, name="ot", tag="ot%d" % j)
                 for g in range(4):
                     nc.tensor.transpose(ot[:, g * P : (g + 1) * P], oo[:, g * P : (g + 1) * P], ident[:])
                 st["ot", s] = ot
 
+        left = [n for first, n in groups]
+
         def stage_c(n):
-            for s in positions(n):
-                c, i = o_of[s]
-                ln = O_CHUNKS[c]
-                if i == 0:
-                    st["ob", c] = [opool.tile([P, 2 * 8 * NF], F32, name="ob%d" % q) for q in range(2)]
-                src = st["ot", s][:].rearrange("p (b h q m) -> p q h m b", b=2, h=2, q=2)
-                for q in range(2):
-                    dst = st["ob", c][q][:, 0 : 2 * ln * NF].rearrange("p (h s m b) -> p h s m b", h=2, s=ln, b=2)
-                    nc.scalar.copy(out=dst[:, :, i, :, :], in_=src[:, q])
-                if i == ln - 1:
-                    first = s - i
+            for s in SLOTS[n]:
+                if not is_edge(s):
+                    nc.scalar.copy(out=out_tile(s).rearrange("p g (m b) -> p g m b", b=2),
+                                   in_=st["ot", s][:].rearrange("p (b g m) -> p g m b", b=2, g=4))
+                g, i = o_of[s]
+                left[g] -= 1
+                if left[g] == 0:
+                    first, cnt = groups[g]
+                    obv = st["ob", g][:].rearrange("p (h q s f) -> p h q s f", h=2, q=2, s=cnt)
                     for q in range(2):
-                        nc.sync.dma_start(
-                            out=ov[q][:, :, first : first + ln, :],
-                            in_=st["ob", c][q][:, 0 : 2 * ln * NF].rearrange("p (h s f) -> p h s f", h=2, s=ln),
-                        )
+                        nc.sync.dma_start(out=ov[q][:, :, first : first + cnt, :], in_=obv[:, :, q])
 
         def run(stage, n):
             if 0 <= n < nslot:
@@ -276,11 +382,16 @@ def tile_attention_pa_t_kernel(tc, x, Wq, bq, Wk, bk, out_0, out_1):
 
         for t in range(-1, nslot + 2):
             run(stage_l, t + 1)
+            if t == -1:
+                for e in range(2):
+                    nc.tensor.transpose(pt2[:, e * P : (e + 1) * P], bab[:, e : e + 1].to_broadcast([P, P]), ident[:])
             run(stage_q, t)
             if t == 0:
                 bias_tables()
             run(stage_a, t - 1)
             run(stage_e, t + 1)
+            if t == 0:
+                edge_tables()
             run(stage_t, t - 2)
             run(stage_b, t - 1)
             run(stage_c, t - 2)

@@ -36,7 +36,7 @@ SLOTS = slot_list()
 X_CHUNKS = [(8, 2), (7, 1), (10, 2), (12, 2), (1, 1), (14, 7), (2, 5), (21, 7), (28, 7), (35, 7), (42, 7), (0, 1)]
 
 
-SCALAR_COPY = {False: (False, True), True: (False, True)}
+SCALAR_COPY = {False: (False, False), True: (True, True)}
 
 
 def is_edge(s):
@@ -159,10 +159,10 @@ def tile_attention_pa_t_kernel(tc, x, Wq, bq, Wk, bk, out_0, out_1):
 
         wg = const.tile([P, 2, P, 4], BF16, name="wg", align_bytes=64)
         for ab in range(2):
-            nc.scalar.copy(
+            nc.scalar.activation(
                 out=wg[:, ab, :, :].rearrange("p (q r) t -> p q r t", q=2),
                 in_=wraw[:].rearrange("p q t (r b) -> p b q r t", b=2)[:, ab],
-            )
+                func=ACT.Identity, scale=1.0 - 2.0 * ab)
         wc = const.tile([P, 2 * P], U32, name="wc", align_bytes=64)
         ws = const.tile([P, 2 * P], U8, name="ws", align_bytes=64)
 
@@ -197,7 +197,7 @@ def tile_attention_pa_t_kernel(tc, x, Wq, bq, Wk, bk, out_0, out_1):
 
         cos_t = const.tile([P, NPOS], F32, name="cos_t")
         sin_t = const.tile([P, NPOS], F32, name="sin_t")
-        nsin_t = const.tile([P, NPOS], F32, name="nsin_t")
+        ncos_t = const.tile([P, NPOS], F32, name="ncos_t")
         bias_a = const.tile([P, NPOS], F32, name="bias_a")
         bias_b = const.tile([P, NPOS], F32, name="bias_b")
         tmp0 = const.tile([P, NPOS], F32, name="tmp0")
@@ -209,7 +209,7 @@ def tile_attention_pa_t_kernel(tc, x, Wq, bq, Wk, bk, out_0, out_1):
             nc.vector.tensor_scalar(out=tv, in0=by_col, scalar1=h01[:, 1:2], scalar2=None, op0=ALU.mult)
             nc.vector.scalar_tensor_tensor(out=dst[:].rearrange("p (r c) -> p r c", c=GRID), in0=by_row,
                                            scalar=h01[:, 0:1], in1=tv, op0=ALU.mult, op1=ALU.add)
-        nc.vector.tensor_scalar(out=nsin_t[:], in0=sin_t[:], scalar1=-1.0, scalar2=None, op0=ALU.mult)
+        nc.vector.tensor_scalar(out=ncos_t[:], in0=cos_t[:], scalar1=-1.0, scalar2=None, op0=ALU.mult)
 
         bab = const.tile([P, 2], F32, name="bab")
         tmp2 = const.tile([P, NPOS], F32, name="tmp2")
@@ -293,10 +293,10 @@ def tile_attention_pa_t_kernel(tc, x, Wq, bq, Wk, bk, out_0, out_1):
                     continue
                 pp = st["pp", s]
                 tt = work.tile([P, 512], F32, name="tt", tag="tt%d" % j)
-                nc.scalar.activation(out=tt[:, 256:512], in_=pp[:, 256:512], func=ACT.Identity,
-                                     bias=bias_b[:, s : s + 1], scale=cos_t[:, s : s + 1])
-                nc.scalar.activation(out=tt[:, 0:256], in_=pp[:, 0:256], func=ACT.Identity,
+                nc.scalar.activation(out=tt[:, 256:512], in_=pp[:, 0:256], func=ACT.Identity,
                                      bias=bias_a[:, s : s + 1], scale=cos_t[:, s : s + 1])
+                nc.scalar.activation(out=tt[:, 0:256], in_=pp[:, 256:512], func=ACT.Identity,
+                                     bias=bias_b[:, s : s + 1], scale=ncos_t[:, s : s + 1])
                 st["tt", s] = tt
 
         def out_tile(s):
@@ -312,10 +312,8 @@ def tile_attention_pa_t_kernel(tc, x, Wq, bq, Wk, bk, out_0, out_1):
                 if not is_edge(s):
                     tt = st["tt", s]
                     oo = work.tile([P, 512], F32, name="oo", tag="oo%d" % j)
-                    nc.vector.scalar_tensor_tensor(out=oo[:, 0:256], in0=pp[:, 256:512], scalar=nsin_t[:, s : s + 1],
-                                                   in1=tt[:, 0:256], op0=ALU.mult, op1=ALU.add)
-                    nc.vector.scalar_tensor_tensor(out=oo[:, 256:512], in0=pp[:, 0:256], scalar=sin_t[:, s : s + 1],
-                                                   in1=tt[:, 256:512], op0=ALU.mult, op1=ALU.add)
+                    nc.vector.scalar_tensor_tensor(out=oo[:], in0=pp[:], scalar=sin_t[:, s : s + 1],
+                                                   in1=tt[:], op0=ALU.mult, op1=ALU.add)
                     st["oo", s] = oo
                     continue
                 ob = out_tile(s)
@@ -358,7 +356,7 @@ def tile_attention_pa_t_kernel(tc, x, Wq, bq, Wk, bk, out_0, out_1):
                 oo = st["oo", s]
                 ot = ps_o.tile([P, 512], F32, name="ot", tag="ot%d" % j)
                 for g in range(4):
-                    nc.tensor.transpose(ot[:, g * P : (g + 1) * P], oo[:, g * P : (g + 1) * P], ident[:])
+                    nc.tensor.transpose(ot[:, (g + 2) % 4 * P : ((g + 2) % 4 + 1) * P], oo[:, g * P : (g + 1) * P], ident[:])
                 st["ot", s] = ot
 
         left = [n for first, n in groups]

@@ -36,7 +36,7 @@ SLOTS = slot_list()
 X_CHUNKS = [(8, 2), (7, 1), (10, 2), (12, 2), (1, 1), (14, 7), (2, 5), (21, 7), (28, 7), (35, 7), (42, 7), (0, 1)]
 
 
-SCALAR_COPY = {False: (False, False), True: (True, True)}
+SCALAR_COPY = {False: (False, True), True: (False, True)}
 
 
 def is_edge(s):
@@ -81,7 +81,7 @@ def tile_attention_pa_t_kernel(tc, x, Wq, bq, Wk, bk, out_0, out_1):
         ctx.enter_context(tc.manual_schedule())
         const = ctx.enter_context(tc.tile_pool(name="const", bufs=1))
         xpool = ctx.enter_context(tc.tile_pool(name="xpool", bufs=1))
-        work = ctx.enter_context(tc.tile_pool(name="work", bufs=2))
+        work = ctx.enter_context(tc.tile_pool(name="work", bufs=3))
         opool = ctx.enter_context(tc.tile_pool(name="opool", bufs=3))
         ps_x = ctx.enter_context(tc.psum_pool(name="ps_x", bufs=1))
         ps_p = ctx.enter_context(tc.psum_pool(name="ps_p", bufs=2))
@@ -303,7 +303,10 @@ def tile_attention_pa_t_kernel(tc, x, Wq, bq, Wk, bk, out_0, out_1):
             g, i = o_of[s]
             n = groups[g][1]
             if ("ob", g) not in st:
-                st["ob", g] = opool.tile([P, 4 * n * NF], F32, name="ob", tag="ob%d_%d" % (n, s < GRID))
+                if s < GRID:
+                    st["ob", g] = const.tile([P, 4 * n * NF], F32, name="ob_row0_%d" % g)
+                else:
+                    st["ob", g] = opool.tile([P, 4 * n * NF], F32, name="ob", tag="ob%d" % n)
             return st["ob", g][:].rearrange("p (g s f) -> p g s f", g=4, s=n)[:, :, i, :]
 
         def stage_b(n):

@@ -83,9 +83,8 @@ def tile_attention_pa_t_kernel(tc, x, Wq, bq, Wk, bk, out_0, out_1):
         xpool = ctx.enter_context(tc.tile_pool(name="xpool", bufs=1))
         work = ctx.enter_context(tc.tile_pool(name="work", bufs=3))
         opool = ctx.enter_context(tc.tile_pool(name="opool", bufs=3))
-        ps_x = ctx.enter_context(tc.psum_pool(name="ps_x", bufs=1))
         ps_p = ctx.enter_context(tc.psum_pool(name="ps_p", bufs=2))
-        ps_o = ctx.enter_context(tc.psum_pool(name="ps_o", bufs=1))
+        ps_t = ctx.enter_context(tc.psum_pool(name="ps_t", bufs=4))
 
         bpair = const.tile([P, 2], BF16, name="bpair")
         for q, b in enumerate((bq, bk)):
@@ -117,7 +116,7 @@ def tile_attention_pa_t_kernel(tc, x, Wq, bq, Wk, bk, out_0, out_1):
                 nc.vector.tensor_scalar(out=col, in0=col, scalar1=val, scalar2=None, op0=ALU.add)
         nc.vector.memset(rw[:, 2, :].rearrange("p (g h j) -> p g h j", h=2, j=8)[:, :, 1, :], 1.0)
 
-        pt = ps_o.tile([P, 512], F32, name="pt", tag="ot0")
+        pt = ps_p.tile([P, 512], F32, name="pt", tag="pp0")
         for v in range(3):
             nc.tensor.transpose(pt[:, v * P : (v + 1) * P], rw[:, v, :], ident[:])
 
@@ -215,7 +214,7 @@ def tile_attention_pa_t_kernel(tc, x, Wq, bq, Wk, bk, out_0, out_1):
         tmp2 = const.tile([P, NPOS], F32, name="tmp2")
         tmp3 = const.tile([P, NPOS], F32, name="tmp3")
         nc.vector.tensor_copy(out=bab[:], in_=bpair[:])
-        pt2 = ps_o.tile([P, 512], F32, name="pt2", tag="ot1")
+        pt2 = ps_p.tile([P, 512], F32, name="pt2", tag="pp1")
         bias_row = const.tile([P, 2, P, 2], F32, name="bias_row")
 
         def bias_tables():
@@ -239,7 +238,7 @@ def tile_attention_pa_t_kernel(tc, x, Wq, bq, Wk, bk, out_0, out_1):
             for j, s in enumerate(SLOTS[n]):
                 c, i = x_of[s]
                 x32 = xs[c][:].bitcast(F32)
-                xt = ps_x.tile([P, 512], F32, name="xt", tag="xt%d" % j)
+                xt = ps_t.tile([P, 512], F32, name="xt", tag="turn")
                 for h in range(2):
                     for u in range(2):
                         off = (h * X_CHUNKS[c][1] + i) * WORDS
@@ -357,7 +356,7 @@ def tile_attention_pa_t_kernel(tc, x, Wq, bq, Wk, bk, out_0, out_1):
                 if is_edge(s):
                     continue
                 oo = st["oo", s]
-                ot = ps_o.tile([P, 512], F32, name="ot", tag="ot%d" % j)
+                ot = ps_t.tile([P, 512], F32, name="ot", tag="turn")
                 for g in range(4):
                     nc.tensor.transpose(ot[:, (g + 2) % 4 * P : ((g + 2) % 4 + 1) * P], oo[:, g * P : (g + 1) * P], ident[:])
                 st["ot", s] = ot

from contextlib import ExitStack

import concourse.bass as bass
import concourse.mybir as mybir
import concourse.tile as tile
from concourse.masks import make_identity

F32 = mybir.dt.float32
BF16 = mybir.dt.bfloat16
U32 = mybir.dt.uint32
U8 = mybir.dt.uint8
FP8X4 = mybir.dt.float8_e4m3fn_x4
ALU = mybir.AluOpType
ACT = mybir.ActivationFunctionType

P = 128
IMAGES = 256
GRID = 7
NPOS = GRID * GRID
E = 512
WORDS = E // 2
NF = 128
BASE = 100.0
FLOPS = 2 * IMAGES * NPOS * E * 2 * NF

def slot_list():
    slots = []
    for row in range(1, GRID):
        s7 = GRID * row
        slots += [(s7 + 1, s7 + 2), (s7 + 3, s7), (s7 + 4, s7 + 5), (s7 + 6, row)]
    return slots + [(0,)]


SLOTS = slot_list()

X_CHUNKS = [(8, 2), (7, 1), (10, 2), (12, 2), (1, 1), (14, 7), (2, 5), (21, 7), (28, 7), (35, 7), (42, 7), (0, 1)]


SCALAR_COPY = {False: (False, True), True: (False, True)}


def is_edge(s):
    return s < GRID or s % GRID == 0


def cos_sin(theta):
    c, s, term = 0.0, 0.0, 1.0
    for n in range(0, 30, 2):
        c += term
        term = term * theta / (n + 1)
        s += term
        term = -term * theta / (n + 2)
    return c, s


def store_groups():
    groups = []
    for row in range(1, GRID):
        groups += [(GRID * row, 4), (GRID * row + 4, 3)]
    groups += [(1, 3), (4, 3), (0, 1)]
    of = {}
    for g, (first, n) in enumerate(groups):
        for i in range(n):
            of[first + i] = (g, i)
    return groups, of


def tile_attention_pa_t_kernel(tc, x, Wq, bq, Wk, bk, out_0, out_1):
    nc = tc.nc
    x_of = {}
    for c, (first, n) in enumerate(X_CHUNKS):
        for i in range(n):
            x_of[first + i] = (c, i)
    groups, o_of = store_groups()
    assert len(x_of) == NPOS and len(o_of) == NPOS
    xv = x.rearrange("(p h) s k -> p h s k", h=2)
    ov = [o.rearrange("(p h) s a d -> p h s (a d)", h=2) for o in (out_0, out_1)]
    nslot = len(SLOTS)

    with ExitStack() as ctx:
        ctx.enter_context(tc.manual_schedule())
        const = ctx.enter_context(tc.tile_pool(name="const", bufs=1))
        xpool = ctx.enter_context(tc.tile_pool(name="xpool", bufs=1))
        work = ctx.enter_context(tc.tile_pool(name="work", bufs=3))
        opool = ctx.enter_context(tc.tile_pool(name="opool", bufs=3))
        ps_p = ctx.enter_context(tc.psum_pool(name="ps_p", bufs=2))
        ps_t = ctx.enter_context(tc.psum_pool(name="ps_t", bufs=4))

        bpair = const.tile([P, 2], BF16, name="bpair")
        for q, b in enumerate((bq, bk)):
            nc.sync.dma_start(out=bpair[64 * q : 64 * (q + 1), :], in_=b.rearrange("(m e) -> m e", e=2))
        wraw = const.tile([P, 2, 4, NF], BF16, name="wraw")
        for q, w in enumerate((Wq, Wk)):
            nc.sync.dma_start(out=wraw[:, q, :, :], in_=w.rearrange("(p t) f -> p t f", t=4))
        xs = []
        for c, (first, n) in enumerate(X_CHUNKS):
            xt_sb = xpool.tile([P, 2 * n * E], BF16, name="xs%d" % c)
            nc.sync.dma_start(
                out=xt_sb[:].rearrange("p (h s k) -> p h s k", h=2, s=n),
                in_=xv[:, :, first : first + n, :],
            )
            xs.append(xt_sb)

        ident = const.tile([P, P], F32, name="ident")
        make_identity(nc, ident[:])
        warm = const.tile([P, 2], F32, name="warm")
        nc.gpsimd.memset(warm[:, 0:1], 0.0)
        nc.scalar.activation(out=warm[:, 1:2], in_=warm[:, 0:1], func=ACT.Identity)

        rw = const.tile([P, 3, P], F32, name="rw")
        nc.vector.memset(rw[:], 0.0)
        for j in range(8):
            theta = BASE ** (-(2.0 * j) / 16.0)
            for v, val in enumerate(cos_sin(theta)):
                col = rw[:, v, :].rearrange("p (g j) -> p g j", j=8)[:, :, j]
                nc.vector.tensor_scalar(out=col, in0=col, scalar1=val, scalar2=None, op0=ALU.add)
        nc.vector.memset(rw[:, 2, :].rearrange("p (g h j) -> p g h j", h=2, j=8)[:, :, 1, :], 1.0)

        pt = ps_p.tile([P, 512], F32, name="pt", tag="pp0")
        for v in range(3):
            nc.tensor.transpose(pt[:, v * P : (v + 1) * P], rw[:, v, :], ident[:])

        wgn = const.tile([P, 2 * NF, 4], BF16, name="wgn", align_bytes=64)
        nc.gpsimd.tensor_scalar(
            out=wgn[:].rearrange("p (q f) t -> p q f t", q=2),
            in0=wraw[:].rearrange("p q t f -> p q f t"),
            scalar1=1.0, scalar2=0.0, op0=ALU.mult, op1=ALU.add)
        wcn = const.tile([P, 2 * P], U32, name="wcn", align_bytes=64)
        wsn = const.tile([P, 2 * P], U8, name="wsn", align_bytes=64)

        gx = const.tile([P, 2, GRID, 8], F32, name="gx")
        nc.gpsimd.memset(gx[:, 0, 0, :], 1.0)
        nc.gpsimd.memset(gx[:, 1, 0, :], 0.0)
        nc.gpsimd.tensor_copy(out=gx[:, :, 1, :], in_=rw[:, 0:2, 0:8])

        def add_angle_free(k, lo, hi):
            n = hi - lo
            prod = []
            for v in range(2):
                t = const.tile([P, 2, 2, 8], F32, name="g%d_%d" % (k, v))
                nc.gpsimd.tensor_tensor(
                    out=t[:, :, 0:n, :], in0=gx[:, :, lo:hi, :],
                    in1=gx[:, v, k, :].unsqueeze(1).unsqueeze(1).to_broadcast([P, 2, n, 8]), op=ALU.mult)
                prod.append(t)
            nc.gpsimd.tensor_tensor(out=gx[:, 0, lo + k : hi + k, :], in0=prod[0][:, 0, 0:n, :],
                                    in1=prod[1][:, 1, 0:n, :], op=ALU.subtract)
            nc.gpsimd.tensor_tensor(out=gx[:, 1, lo + k : hi + k, :], in0=prod[0][:, 1, 0:n, :],
                                    in1=prod[1][:, 0, 0:n, :], op=ALU.add)

        add_angle_free(1, 1, 2)
        add_angle_free(2, 1, 3)
        add_angle_free(4, 1, 3)
        cx = const.tile([P, GRID, 8, 2], F32, name="cx")
        sx = const.tile([P, GRID, 8, 2], F32, name="sx")
        nc.gpsimd.tensor_copy(out=cx[:], in_=gx[:, 0].unsqueeze(3).to_broadcast([P, GRID, 8, 2]))
        nc.gpsimd.tensor_scalar(out=sx[:, :, :, 0], in0=gx[:, 1], scalar1=-1.0, scalar2=None, op0=ALU.mult)
        nc.gpsimd.tensor_copy(out=sx[:, :, :, 1], in_=gx[:, 1])

        wg = const.tile([P, 2, P, 4], BF16, name="wg", align_bytes=64)
        for ab in range(2):
            nc.scalar.activation(
                out=wg[:, ab, :, :].rearrange("p (q r) t -> p q r t", q=2),
                in_=wraw[:].rearrange("p q t (r b) -> p b q r t", b=2)[:, ab],
                func=ACT.Identity, scale=1.0 - 2.0 * ab)
        wc = const.tile([P, 2 * P], U32, name="wc", align_bytes=64)
        ws = const.tile([P, 2 * P], U8, name="ws", align_bytes=64)

        tcs = const.tile([P, 2, GRID], F32, name="tcs")
        h01 = const.tile([P, 2], F32, name="h01")
        nc.vector.memset(tcs[:, 0, 0:1], 1.0)
        nc.vector.memset(tcs[:, 1, 0:1], 0.0)
        ptv = pt[:].rearrange("p (v n) -> p v n", n=P)
        nc.vector.tensor_copy(out=tcs[:, :, 1], in_=ptv[:, 0:2, 0])
        nc.vector.tensor_copy(out=h01[:, 1:2], in_=ptv[:, 2, 0:1])
        nc.vector.tensor_scalar(out=h01[:, 0:1], in0=h01[:, 1:2], scalar1=-1.0, scalar2=1.0,
                                op0=ALU.mult, op1=ALU.add)

        def add_angle(k, lo, hi):
            ck = tcs[:, 0, k : k + 1]
            sk = tcs[:, 1, k : k + 1]
            n = hi - lo
            u = const.tile([P, 2, 2], F32, name="u%d" % k)
            nc.vector.tensor_scalar(out=u[:, :, 0:n], in0=tcs[:, :, lo:hi], scalar1=sk, scalar2=None,
                                    op0=ALU.mult)
            nc.vector.scalar_tensor_tensor(out=tcs[:, 0, lo + k : hi + k], in0=tcs[:, 0, lo:hi], scalar=ck,
                                           in1=u[:, 1, 0:n], op0=ALU.mult, op1=ALU.subtract)
            nc.vector.scalar_tensor_tensor(out=tcs[:, 1, lo + k : hi + k], in0=tcs[:, 1, lo:hi], scalar=ck,
                                           in1=u[:, 0, 0:n], op0=ALU.mult, op1=ALU.add)

        add_angle(1, 1, 2)
        add_angle(2, 1, 3)
        add_angle(4, 1, 3)

        nc.vector.quantize_mx(out=wc[:].bitcast(FP8X4), scales=ws[:],
                              in_=wg[:].rearrange("p b m t -> p (b m t)"))

        cos_t = const.tile([P, NPOS], F32, name="cos_t")
        sin_t = const.tile([P, NPOS], F32, name="sin_t")
        ncos_t = const.tile([P, NPOS], F32, name="ncos_t")
        bias_a = const.tile([P, NPOS], F32, name="bias_a")
        bias_b = const.tile([P, NPOS], F32, name="bias_b")
        tmp0 = const.tile([P, NPOS], F32, name="tmp0")
        tmp1 = const.tile([P, NPOS], F32, name="tmp1")
        for v, (dst, tmp) in enumerate(((cos_t, tmp0), (sin_t, tmp1))):
            by_col = tcs[:, v, :].unsqueeze(1).to_broadcast([P, GRID, GRID])
            by_row = tcs[:, v, :].unsqueeze(2).to_broadcast([P, GRID, GRID])
            tv = tmp[:].rearrange("p (r c) -> p r c", c=GRID)
            nc.vector.tensor_scalar(out=tv, in0=by_col, scalar1=h01[:, 1:2], scalar2=None, op0=ALU.mult)
            nc.vector.scalar_tensor_tensor(out=dst[:].rearrange("p (r c) -> p r c", c=GRID), in0=by_row,
                                           scalar=h01[:, 0:1], in1=tv, op0=ALU.mult, op1=ALU.add)
        nc.vector.tensor_scalar(out=ncos_t[:], in0=cos_t[:], scalar1=-1.0, scalar2=None, op0=ALU.mult)

        bab = const.tile([P, 2], F32, name="bab")
        tmp2 = const.tile([P, NPOS], F32, name="tmp2")
        tmp3 = const.tile([P, NPOS], F32, name="tmp3")
        nc.vector.tensor_copy(out=bab[:], in_=bpair[:])
        pt2 = ps_p.tile([P, 512], F32, name="pt2", tag="pp1")
        bias_row = const.tile([P, 2, P, 2], F32, name="bias_row")

        def bias_tables():
            nc.vector.tensor_scalar(out=tmp2[:], in0=sin_t[:], scalar1=bab[:, 1:2], scalar2=None, op0=ALU.mult)
            nc.vector.scalar_tensor_tensor(out=bias_a[:], in0=cos_t[:], scalar=bab[:, 0:1], in1=tmp2[:],
                                           op0=ALU.mult, op1=ALU.subtract)
            nc.vector.tensor_scalar(out=tmp3[:], in0=cos_t[:], scalar1=bab[:, 1:2], scalar2=None, op0=ALU.mult)
            nc.vector.scalar_tensor_tensor(out=bias_b[:], in0=sin_t[:], scalar=bab[:, 0:1], in1=tmp3[:],
                                           op0=ALU.mult, op1=ALU.add)

        def edge_tables():
            nc.vector.quantize_mx(out=wcn[:].bitcast(FP8X4), scales=wsn[:],
                                  in_=wgn[:].rearrange("p f t -> p (f t)"))
            nc.vector.tensor_copy(
                out=bias_row[:],
                in_=pt2[:, 0 : 2 * P].rearrange("p (e m) -> p m e", e=2).unsqueeze(1).to_broadcast([P, 2, P, 2]))

        st = {}

        def stage_l(n):
            for j, s in enumerate(SLOTS[n]):
                c, i = x_of[s]
                x32 = xs[c][:].bitcast(F32)
                xt = ps_t.tile([P, 512], F32, name="xt", tag="turn")
                for h in range(2):
                    for u in range(2):
                        off = (h * X_CHUNKS[c][1] + i) * WORDS
                        nc.tensor.transpose(xt[:, (2 * h + u) * P : (2 * h + u + 1) * P],
                                            x32[:, off + u : off + WORDS : 2], ident[:])
                st["xt", s] = xt

        def on_scalar(n, j):
            if n == 0:
                return True
            return SCALAR_COPY[any(is_edge(s) for s in SLOTS[n])][j]

        def stage_e(n):
            xg = work.tile([P, 2048], BF16, name="xg", align_bytes=64)
            st["xg", n] = xg
            for j, s in enumerate(SLOTS[n]):
                dst = xg[:, j * 1024 : (j + 1) * 1024].bitcast(F32).rearrange("p (h i u) -> p h i u", h=2, u=2)
                src = st["xt", s][:].rearrange("p (h u i) -> p h i u", h=2, u=2)
                if on_scalar(n, j):
                    nc.scalar.copy(out=dst, in_=src)
                else:
                    nc.vector.tensor_copy(out=dst, in_=src)

        def stage_q(n):
            w = 256 * len(SLOTS[n])
            xc = work.tile([P, 512], U32, name="xc", align_bytes=64)
            xsc = work.tile([P, 512], U8, name="xsc", align_bytes=64)
            nc.vector.quantize_mx(out=xc[:, 0:w].bitcast(FP8X4), scales=xsc[:, 0:w], in_=st["xg", n][:, 0 : 4 * w])
            st["xc", n] = (xc, xsc)

        def stage_m(n):
            xc, xsc = st["xc", n]
            for j, s in enumerate(SLOTS[n]):
                pp = ps_p.tile([P, 512], F32, name="pp", tag="pp%d" % j)
                for g in range(2):
                    if is_edge(s):
                        cols = slice(j * 256 + g * P, j * 256 + (g + 1) * P)
                        lhs, lhs_s = xc[:, cols], xsc[:, cols]
                        rhs, rhs_s = wcn[:], wsn[:]
                    else:
                        cols = slice(j * 256, (j + 1) * 256)
                        lhs, lhs_s = wc[:, g * P : (g + 1) * P], ws[:, g * P : (g + 1) * P]
                        rhs, rhs_s = xc[:, cols], xsc[:, cols]
                    nc.tensor.matmul_mx(out=pp[:, g * 256 : (g + 1) * 256], lhsT=lhs.bitcast(FP8X4), lhsT_scale=lhs_s,
                                        rhs=rhs.bitcast(FP8X4), rhs_scale=rhs_s, start=True, stop=True)
                st["pp", s] = pp

        def stage_a(n):
            for j, s in enumerate(SLOTS[n]):
                if is_edge(s):
                    continue
                pp = st["pp", s]
                tt = work.tile([P, 512], F32, name="tt", tag="tt%d" % j)
                nc.scalar.activation(out=tt[:, 256:512], in_=pp[:, 0:256], func=ACT.Identity,
                                     bias=bias_a[:, s : s + 1], scale=cos_t[:, s : s + 1])
                nc.scalar.activation(out=tt[:, 0:256], in_=pp[:, 256:512], func=ACT.Identity,
                                     bias=bias_b[:, s : s + 1], scale=ncos_t[:, s : s + 1])
                st["tt", s] = tt

        def out_tile(s):
            g, i = o_of[s]
            n = groups[g][1]
            if ("ob", g) not in st:
                if s < GRID:
                    st["ob", g] = const.tile([P, 4 * n * NF], F32, name="ob_row0_%d" % g)
                else:
                    st["ob", g] = opool.tile([P, 4 * n * NF], F32, name="ob", tag="ob%d" % n)
            return st["ob", g][:].rearrange("p (g s f) -> p g s f", g=4, s=n)[:, :, i, :]

        def stage_b(n):
            for j, s in enumerate(SLOTS[n]):
                pp = st["pp", s]
                if not is_edge(s):
                    tt = st["tt", s]
                    oo = work.tile([P, 512], F32, name="oo", tag="oo%d" % j)
                    nc.vector.scalar_tensor_tensor(out=oo[:], in0=pp[:], scalar=sin_t[:, s : s + 1],
                                                   in1=tt[:], op0=ALU.mult, op1=ALU.add)
                    st["oo", s] = oo
                    continue
                ob = out_tile(s)
                brow = bias_row[:].rearrange("p h m e -> p (h m e)")
                if s == 0:
                    nc.vector.tensor_tensor(out=ob, in0=pp[:].rearrange("p (g f) -> p g f", g=4),
                                            in1=brow.rearrange("p (g f) -> p g f", g=4), op=ALU.add)
                    continue
                rot = 1 if s < GRID else 0
                angle = s if s < GRID else s // GRID
                zr = work.tile([P, 256], F32, name="zr")
                nc.vector.tensor_tensor(
                    out=zr[:].rearrange("p (g f) -> p g f", f=16),
                    in0=pp[:].rearrange("p (g v f) -> p g v f", v=2, f=16)[:, :, rot, :],
                    in1=brow.rearrange("p (g v f) -> p g v f", v=2, f=16)[:, :, rot, :], op=ALU.add)
                obv = ob.rearrange("p g (a v f) -> p g a v f", v=2, f=16)
                nc.vector.tensor_tensor(
                    out=obv[:, :, :, 1 - rot, :],
                    in0=pp[:].rearrange("p (g a v f) -> p g a v f", g=4, v=2, f=16)[:, :, :, 1 - rot, :],
                    in1=brow.rearrange("p (g a v f) -> p g a v f", g=4, v=2, f=16)[:, :, :, 1 - rot, :], op=ALU.add)
                t1 = work.tile([P, 256], F32, name="t1")
                t2 = work.tile([P, 256], F32, name="t2")
                nc.gpsimd.tensor_tensor(
                    out=t1[:].rearrange("p (g f) -> p g f", f=16),
                    in0=zr[:].rearrange("p (g f) -> p g f", f=16),
                    in1=cx[:, angle].rearrange("p j e -> p (j e)").unsqueeze(1).to_broadcast([P, 16, 16]), op=ALU.mult)
                nc.gpsimd.tensor_tensor(
                    out=t2[:].rearrange("p (g j e) -> p g j e", j=8, e=2),
                    in0=zr[:].rearrange("p (g j e) -> p g j e", j=8, e=2)[:, :, :, ::-1],
                    in1=sx[:, angle].unsqueeze(1).to_broadcast([P, 16, 8, 2]), op=ALU.mult)
                nc.gpsimd.tensor_tensor(
                    out=obv[:, :, :, rot, :],
                    in0=t1[:].rearrange("p (g a f) -> p g a f", g=4, f=16),
                    in1=t2[:].rearrange("p (g a f) -> p g a f", g=4, f=16), op=ALU.add)

        def stage_t(n):
            for j, s in enumerate(SLOTS[n]):
                if is_edge(s):
                    continue
                oo = st["oo", s]
                ot = ps_t.tile([P, 512], F32, name="ot", tag="turn")
                for g in range(4):
                    nc.tensor.transpose(ot[:, (g + 2) % 4 * P : ((g + 2) % 4 + 1) * P], oo[:, g * P : (g + 1) * P], ident[:])
                st["ot", s] = ot

        left = [n for first, n in groups]

        def stage_c(n):
            for s in SLOTS[n]:
                if not is_edge(s):
                    nc.scalar.copy(out=out_tile(s).rearrange("p g (m b) -> p g m b", b=2),
                                   in_=st["ot", s][:].rearrange("p (b g m) -> p g m b", b=2, g=4))
                g, i = o_of[s]
                left[g] -= 1
                if left[g] == 0:
                    first, cnt = groups[g]
                    obv = st["ob", g][:].rearrange("p (h q s f) -> p h q s f", h=2, q=2, s=cnt)
                    for q in range(2):
                        nc.sync.dma_start(out=ov[q][:, :, first : first + cnt, :], in_=obv[:, :, q])

        def run(stage, n):
            if 0 <= n < nslot:
                stage(n)

        for t in range(-1, nslot + 2):
            run(stage_l, t + 1)
            if t == -1:
                for e in range(2):
                    nc.tensor.transpose(pt2[:, e * P : (e + 1) * P], bab[:, e : e + 1].to_broadcast([P, P]), ident[:])
            run(stage_q, t)
            if t == 0:
                bias_tables()
            run(stage_a, t - 1)
            run(stage_e, t + 1)
            if t == 0:
                edge_tables()
            run(stage_t, t - 2)
            run(stage_b, t - 1)
            run(stage_c, t - 2)
            run(stage_m, t)
